import numpy as np
import ml_dtypes


def mxq(x, axis, fmt="e4m3"):
    dtype, down = {"e4m3": (ml_dtypes.float8_e4m3fn, 7), "e5m2": (ml_dtypes.float8_e5m2, 14)}[fmt]
    v = np.moveaxis(np.asarray(x, np.float32).astype(ml_dtypes.bfloat16).astype(np.float64), axis, -1)
    blocks = v.reshape(v.shape[:-1] + (-1, 32))
    amax = np.abs(blocks).max(-1, keepdims=True)
    byte = np.maximum(np.where(amax > 0, np.frexp(amax)[1] - 1 + 127, 0) - down, 1)
    scale = np.exp2(byte - 127.0)
    codes = (blocks / scale).astype(np.float32).astype(dtype).astype(np.float64)
    return np.moveaxis((codes * scale).reshape(v.shape), -1, axis)


WIDE = False


def mx_kscale(k):
    if not WIDE:
        return np.ones(k)
    levels = np.array([10, -10, 5, -5, 0])
    if k % 512:
        return np.exp2(np.random.permutation(np.resize(levels, k // 32))).repeat(32)
    a = np.empty((k // 512, 16))
    for p in range(k // 512):
        a[p, :8] = np.random.permutation(np.resize(levels, 8))
        for g in range(8):
            far = levels[np.abs(levels - a[p, g]) >= 10]
            a[p, g + 8] = far[np.random.randint(len(far))]
    return np.exp2(a.ravel()).repeat(32)


BF16 = ml_dtypes.bfloat16


def bf(x):
    return np.asarray(x, np.float32).astype(BF16)


def f64(x):
    return np.asarray(x).astype(np.float64)


E2M1 = np.array([0.0, 0.5, 1.0, 1.5, 2.0, 3.0, 4.0, 6.0, -0.0, -0.5, -1.0, -1.5, -2.0, -3.0, -4.0, -6.0])


def pack_weight(w, fmt):
    k, n = w.shape
    w = f64(bf(w)).reshape(k // 32, 32, n)
    amax = np.abs(w).max(1)
    if fmt == "e4m3":
        byte = np.frexp(amax)[1] - 1 + 127 - 7
    else:
        mant, ex = np.frexp(amax / 6.0)
        byte = np.where(mant > 0.5, ex, ex - 1) + 127
    byte = np.clip(np.where(amax > 0, byte, 1), 1, 254)
    scaled = (w * np.exp2(127.0 - byte)[:, None, :]).reshape(k, n).astype(np.float32)
    by_word = np.ascontiguousarray(scaled.reshape(k // 512, 128, 4, n).transpose(0, 1, 3, 2))
    if fmt == "e4m3":
        words = by_word.astype(ml_dtypes.float8_e4m3fn).view(np.uint8)
    else:
        c = by_word.astype(ml_dtypes.float4_e2m1fn).view(np.uint8) & 0xF
        words = c[..., 0::2] | (c[..., 1::2] << 4)
    return np.ascontiguousarray(words), np.ascontiguousarray(byte.astype(np.uint8).reshape(k // 512, 16, n))


def unpack_weight(words, scales, fmt):
    g, p, n, _ = words.shape
    if fmt == "e4m3":
        vals = np.ascontiguousarray(words).view(ml_dtypes.float8_e4m3fn).astype(np.float64)
    else:
        nib = np.empty((g, p, n, 4), np.uint8)
        nib[..., 0::2] = words & 0xF
        nib[..., 1::2] = words >> 4
        vals = E2M1[nib]
    vals = vals * np.repeat(np.exp2(scales.astype(np.float64) - 127.0), 8, axis=1)[..., None]
    return vals.transpose(0, 1, 3, 2).reshape(g * 512, n)


B, C, H, W, O, KH, KW, PH, PW, T, R = 4, 256, 31, 32, 256, 2, 1, 1, 0, 8, 64
HO, WO = H + PH + PH - KH + 1, W + PW + PW - KW + 1
N = B * HO * WO
D = C * KH * KW
R2 = R * KH * KW
K1, K2 = T * R, T * R2
FMT = "e4m3"


def setup_inputs():
    s, t1, t2 = mx_kscale(D), mx_kscale(K1).reshape(T, R), mx_kscale(K2).reshape(T, R2)
    xw = bf(np.random.standard_normal((N, D)) * s)
    s1_stack = np.random.standard_normal((T, D, R)) / np.sqrt(D) / s[None, :, None] * t1[:, None, :]
    S1s_words, S1s_scales = pack_weight(s1_stack.reshape(-1, R), FMT)
    U1s = bf(np.random.standard_normal((T, R, O)) * T / np.sqrt(K1) / t1[:, :, None])
    u2_stack = np.random.standard_normal((T, R2, D)) / np.sqrt(D) / s[None, None, :] * t2[:, :, None]
    U2s_words, U2s_scales = pack_weight(u2_stack.swapaxes(1, 2).reshape(-1, R2), FMT)
    S2s = bf(np.random.standard_normal((T, R2, O)) * T / np.sqrt(K2) / t2[:, :, None])
    bias = bf(np.random.standard_normal(O) * 0.3)
    return {"xw": xw,
            "S1s_words": S1s_words, "S1s_scales": S1s_scales,
            "U1s": U1s,
            "U2s_words": U2s_words, "U2s_scales": U2s_scales,
            "S2s": S2s,
            "bias": bias}


def reference(xw, S1s_words, S1s_scales, U1s, U2s_words, U2s_scales, S2s, bias):
    xq = mxq(f64(xw), 1, "e4m3")
    s1 = unpack_weight(S1s_words, S1s_scales, FMT).reshape(T, D, R).transpose(1, 0, 2).reshape(D, K1)
    h1 = xq @ s1
    out1 = (mxq(h1, 1, "e4m3") @ mxq(f64(U1s).reshape(K1, O), 0, "e4m3")) / T + f64(bias)
    u2t = unpack_weight(U2s_words, U2s_scales, FMT).reshape(T, D, R2).transpose(1, 0, 2).reshape(D, K2)
    h2 = xq @ u2t
    out2 = (mxq(h2, 1, "e4m3") @ mxq(f64(S2s).reshape(K2, O), 0, "e4m3")) / T
    out = out1 + out2 + f64(bias)
    return out.reshape(B, HO, WO, O).transpose(0, 3, 1, 2)

@@ -1,0 +1,259 @@
+from contextlib import ExitStack
+
+import concourse.mybir as mybir
+from concourse.masks import make_identity
+
+F32 = mybir.dt.float32
+BF16 = mybir.dt.bfloat16
+I32 = mybir.dt.int32
+U32 = mybir.dt.uint32
+U8 = mybir.dt.uint8
+FP8X4 = mybir.dt.float8_e4m3fn_x4
+IDENTITY = mybir.ActivationFunctionType.Identity
+
+P = 128
+PACK = 4
+K_PASS = P * PACK
+
+WINDOWS = 4096
+D = 512
+TERMS = 8
+H1 = 512
+HIDDEN = 1536
+HIDDEN_PASSES = HIDDEN // K_PASS
+OUT_CH = 256
+OUT_TILES = OUT_CH // P
+IMAGE = 1024
+
+GROUP = 512
+GROUPS = WINDOWS // GROUP
+PIECE = 128
+PIECES = GROUP // PIECE
+HALVES = 2
+HALF = GROUP // HALVES
+SCALE_ROWS = 4
+QUADRANTS = 4
+
+FLOPS = 2 * WINDOWS * D * HIDDEN + 2 * WINDOWS * HIDDEN * OUT_CH
+
+
+def tile_skconv2d_pa_t_e_kernel(
+    tc, xw, S1s_words, S1s_scales, U1s, U2s_words, U2s_scales, S2s, bias, out
+):
+    nc = tc.nc
+    with ExitStack() as ctx:
+        const = ctx.enter_context(tc.tile_pool(name="const", bufs=1))
+        x_pool = ctx.enter_context(tc.tile_pool(name="x_rows", bufs=GROUPS * HALVES))
+        pair = ctx.enter_context(tc.tile_pool(name="pair", bufs=2))
+        hg_pool = ctx.enter_context(tc.tile_pool(name="h_grouped", bufs=3))
+        y_pool = ctx.enter_context(tc.tile_pool(name="y", bufs=4))
+        h_psum = ctx.enter_context(tc.psum_pool(name="h_psum", bufs=6))
+        side_psum = ctx.enter_context(tc.psum_pool(name="side_psum", bufs=2))
+        ctx.enter_context(tc.manual_schedule())
+
+        ident = const.tile([P, P], F32)
+        make_identity(nc, ident[:])
+
+        w1_words_raw = const.tile([P, HIDDEN], I32, align_bytes=64)
+        w1_scales_raw = const.tile([P, HIDDEN], U8, align_bytes=64)
+        nc.vector.memset(w1_scales_raw[:].bitcast(I32), 0)
+        w1_words = const.tile([P, HIDDEN], I32, align_bytes=64)
+        w1_scales = const.tile([P, HIDDEN], U8, align_bytes=64)
+
+        def permute_stage1_weights(c):
+            cols = slice(K_PASS * c, K_PASS * (c + 1))
+            for permuted, raw in ((w1_words, w1_words_raw), (w1_scales, w1_scales_raw)):
+                nc.vector.tensor_copy(
+                    out=permuted[:, cols].rearrange("p (j m) -> p j m", j=PACK),
+                    in_=raw[:, cols].rearrange("p (m j) -> p j m", j=PACK),
+                )
+
+        bias_cols = const.tile([P, OUT_TILES], BF16)
+        with nc.allow_non_contiguous_dma(reason="256 bias values, one per partition and tile"):
+            nc.sync.dma_start(out=bias_cols[:], in_=bias.rearrange("(t p) -> p t", p=P))
+
+        x_rows = {}
+
+        def load_x(g):
+            for half in range(HALVES):
+                first = GROUP * g + HALF * half
+                rows = x_pool.tile([P, HALF // P, D], BF16, name="x_rows")
+                nc.sync.dma_start(
+                    out=rows[:], in_=xw[first : first + HALF, :].rearrange("(s p) d -> p s d", p=P)
+                )
+                x_rows[(g, half)] = rows
+
+        def load_stage1_weights(words, scales, first, count):
+            cols = slice(first, first + count)
+            nc.sync.dma_start(
+                out=w1_words_raw[:, cols].rearrange("p (g n) -> p g n", g=TERMS),
+                in_=words.rearrange("g p n t -> p g (n t)").bitcast(I32),
+            )
+            for quadrant in range(QUADRANTS):
+                nc.sync.dma_start(
+                    out=w1_scales_raw[32 * quadrant : 32 * quadrant + SCALE_ROWS, cols]
+                    .bitcast(I32)
+                    .rearrange("r (g n) -> r g n", g=TERMS),
+                    in_=scales[:, SCALE_ROWS * quadrant : SCALE_ROWS * (quadrant + 1), :]
+                    .rearrange("g r n -> r g n")
+                    .bitcast(I32),
+                )
+
+        w2_raw = const.tile([P, HIDDEN // P, OUT_CH], BF16)
+
+        load_x(0)
+        load_stage1_weights(S1s_words, S1s_scales, 0, H1)
+        load_x(1)
+        load_stage1_weights(U2s_words, U2s_scales, H1, HIDDEN - H1)
+        nc.sync.dma_start(
+            out=w2_raw[:, 0 : H1 // P, :],
+            in_=U1s.rearrange("t r o -> (t r) o").rearrange("(p j) o -> p j o", j=PACK),
+        )
+        nc.sync.dma_start(
+            out=w2_raw[:, H1 // P :, :].rearrange("p (c j) o -> p c j o", j=PACK),
+            in_=S2s.rearrange("t r o -> (t r) o").rearrange("(c p j) o -> p c j o", p=P, j=PACK),
+        )
+        for g in range(2, GROUPS):
+            load_x(g)
+
+        bias2 = const.tile([P, OUT_TILES], F32)
+        nc.scalar.activation(out=bias2[:], in_=bias_cols[:], func=IDENTITY, scale=2.0)
+
+        w2_grouped = const.tile([P, HIDDEN_PASSES, OUT_CH, PACK], BF16, align_bytes=64)
+        w2_words = const.tile([P, HIDDEN_PASSES, OUT_CH], U32, align_bytes=64)
+        w2_scales = const.tile([P, HIDDEN_PASSES, OUT_CH], U8, align_bytes=64)
+
+        def quantise_stage2_weights():
+            for c in range(HIDDEN_PASSES):
+                copy = nc.scalar.copy if c < HIDDEN_PASSES - 1 else nc.vector.tensor_copy
+                copy(
+                    out=w2_grouped[:, c],
+                    in_=w2_raw[:, PACK * c : PACK * (c + 1), :].rearrange("p j o -> p o j"),
+                )
+            for c in range(HIDDEN_PASSES):
+                nc.vector.quantize_mx(
+                    out=w2_words[:, c, :].bitcast(FP8X4),
+                    scales=w2_scales[:, c, :],
+                    in_=w2_grouped[:, c].rearrange("p o j -> p (o j)"),
+                )
+
+        x_grouped = {}
+        x_words = {}
+        x_scales = {}
+        h_grouped = {}
+        h_words = {}
+        h_scales = {}
+
+        def transpose_x(g):
+            grouped = pair.tile([P, GROUP * PACK], BF16, align_bytes=64, name="x_grouped")
+            grouped_words = grouped[:].bitcast(F32).rearrange("p (w u) -> p w u", u=2)
+            for half in range(HALVES):
+                xt = side_psum.tile([P, 2, HALF], F32, name="xt", tag="side")
+                for s in range(HALF // P):
+                    words = x_rows[(g, half)][:, s, :].bitcast(F32)
+                    for u in range(2):
+                        nc.tensor.transpose(
+                            xt[:, u, P * s : P * (s + 1)], words[:, u : D // 2 : 2], ident[:]
+                        )
+                nc.scalar.copy(
+                    out=grouped_words[:, HALF * half : HALF * (half + 1), :],
+                    in_=xt[:].rearrange("p u w -> p w u"),
+                )
+            x_grouped[g] = grouped
+
+        def quantise_x(g):
+            words = pair.tile([P, GROUP], U32, align_bytes=64, name="x_words")
+            scales = pair.tile([P, GROUP], U8, align_bytes=64, name="x_scales")
+            for half in range(HALVES):
+                windows = slice(HALF * half, HALF * (half + 1))
+                nc.vector.quantize_mx(
+                    out=words[:, windows].bitcast(FP8X4),
+                    scales=scales[:, windows],
+                    in_=x_grouped[g][:, PACK * HALF * half : PACK * HALF * (half + 1)],
+                )
+            x_words[g] = words
+            x_scales[g] = scales
+
+        def stage1(g, c):
+            grouped = hg_pool.tile([P, GROUP, PACK], BF16, align_bytes=64, name="h_grouped")
+            for q in range(PIECES):
+                windows = slice(PIECE * q, PIECE * (q + 1))
+                h_bank = h_psum.tile([P, PACK, PIECE], F32, name="h_bank")
+                for j in range(PACK):
+                    rows = slice(K_PASS * c + P * j, K_PASS * c + P * (j + 1))
+                    nc.tensor.matmul_mx(
+                        out=h_bank[:, j, :],
+                        lhsT=w1_words[:, rows].bitcast(FP8X4),
+                        lhsT_scale=w1_scales[:, rows],
+                        rhs=x_words[g][:, windows].bitcast(FP8X4),
+                        rhs_scale=x_scales[g][:, windows],
+                        start=True,
+                        stop=True,
+                    )
+                copy = nc.scalar.copy if q % 2 == 0 else nc.vector.tensor_copy
+                copy(out=grouped[:, windows, :], in_=h_bank[:].rearrange("p j w -> p w j"))
+            h_grouped[(g, c)] = grouped
+
+        def quantise_h(g, c):
+            if c == 0:
+                words = pair.tile([P, HIDDEN_PASSES, GROUP], U32, align_bytes=64, name="h_words")
+                scales = pair.tile([P, HIDDEN_PASSES, GROUP], U8, align_bytes=64, name="h_scales")
+                h_words[g] = words
+                h_scales[g] = scales
+            nc.vector.quantize_mx(
+                out=h_words[g][:, c, :].bitcast(FP8X4),
+                scales=h_scales[g][:, c, :],
+                in_=h_grouped[(g, c)][:].rearrange("p w j -> p (w j)"),
+            )
+
+        out_rows = out.rearrange("b o i j -> b o (i j)")
+
+        def stage2(g, t):
+            image = GROUP * g // IMAGE
+            first = GROUP * g % IMAGE
+            channels = slice(P * t, P * (t + 1))
+            y_bank = side_psum.tile([P, GROUP], F32, name="y_bank", tag="side")
+            for c in range(HIDDEN_PASSES):
+                nc.tensor.matmul_mx(
+                    out=y_bank[:],
+                    lhsT=w2_words[:, c, channels].bitcast(FP8X4),
+                    lhsT_scale=w2_scales[:, c, channels],
+                    rhs=h_words[g][:, c, :].bitcast(FP8X4),
+                    rhs_scale=h_scales[g][:, c, :],
+                    start=(c == 0),
+                    stop=(c == HIDDEN_PASSES - 1),
+                )
+            y_sb = y_pool.tile([P, GROUP], F32, name="y_sb")
+            nc.scalar.activation(
+                out=y_sb[:], in_=y_bank[:], func=IDENTITY, bias=bias2[:, t : t + 1], scale=1.0 / TERMS
+            )
+            nc.sync.dma_start(out=out_rows[image, channels, first : first + GROUP], in_=y_sb[:])
+
+        transpose_x(0)
+        permute_stage1_weights(0)
+        quantise_x(0)
+        for g in range(GROUPS):
+            stage1(g, 0)
+            if g == 0:
+                permute_stage1_weights(1)
+            if g > 0:
+                quantise_h(g - 1, 2)
+            if g + 1 < GROUPS:
+                transpose_x(g + 1)
+            stage1(g, 1)
+            if g == 0:
+                permute_stage1_weights(2)
+            quantise_h(g, 0)
+            if g + 1 < GROUPS:
+                quantise_x(g + 1)
+            if g > 0:
+                stage2(g - 1, 0)
+            stage1(g, 2)
+            quantise_h(g, 1)
+            if g > 0:
+                stage2(g - 1, 1)
+            else:
+                quantise_stage2_weights()
+        quantise_h(GROUPS - 1, 2)
+        stage2(GROUPS - 1, 0)
+        stage2(GROUPS - 1, 1)

@@ -10,6 +10,8 @@ U32 = mybir.dt.uint32
 U8 = mybir.dt.uint8
 FP8X4 = mybir.dt.float8_e4m3fn_x4
 IDENTITY = mybir.ActivationFunctionType.Identity
+MULT = mybir.AluOpType.mult
+ADD = mybir.AluOpType.add
 
 P = 128
 PACK = 4
@@ -18,7 +20,7 @@ K_PASS = P * PACK
 WINDOWS = 4096
 D = 512
 TERMS = 8
-H1 = 512
+H2 = 1024
 HIDDEN = 1536
 HIDDEN_PASSES = HIDDEN // K_PASS
 OUT_CH = 256
@@ -29,8 +31,7 @@ GROUP = 512
 GROUPS = WINDOWS // GROUP
 PIECE = 128
 PIECES = GROUP // PIECE
-HALVES = 2
-HALF = GROUP // HALVES
+HALF = GROUP // 2
 SCALE_ROWS = 4
 QUADRANTS = 4
 
@@ -43,10 +44,10 @@ def tile_skconv2d_pa_t_e_kernel(
     nc = tc.nc
     with ExitStack() as ctx:
         const = ctx.enter_context(tc.tile_pool(name="const", bufs=1))
-        x_pool = ctx.enter_context(tc.tile_pool(name="x_rows", bufs=GROUPS * HALVES))
-        pair = ctx.enter_context(tc.tile_pool(name="pair", bufs=2))
-        hg_pool = ctx.enter_context(tc.tile_pool(name="h_grouped", bufs=3))
-        y_pool = ctx.enter_context(tc.tile_pool(name="y", bufs=4))
+        x_pool = ctx.enter_context(tc.tile_pool(name="x_rows", bufs=2 * GROUPS + 1))
+        stage = ctx.enter_context(tc.tile_pool(name="stage", bufs=4))
+        hg_pool = ctx.enter_context(tc.tile_pool(name="h_grouped", bufs=9))
+        y_pool = ctx.enter_context(tc.tile_pool(name="y", bufs=8))
         h_psum = ctx.enter_context(tc.psum_pool(name="h_psum", bufs=6))
         side_psum = ctx.enter_context(tc.psum_pool(name="side_psum", bufs=2))
         ctx.enter_context(tc.manual_schedule())
@@ -60,35 +61,42 @@ def tile_skconv2d_pa_t_e_kernel(
         w1_words = const.tile([P, HIDDEN], I32, align_bytes=64)
         w1_scales = const.tile([P, HIDDEN], U8, align_bytes=64)
 
-        def permute_stage1_weights(c):
+        def permute_columns(permuted, raw, c):
             cols = slice(K_PASS * c, K_PASS * (c + 1))
-            for permuted, raw in ((w1_words, w1_words_raw), (w1_scales, w1_scales_raw)):
-                nc.vector.tensor_copy(
-                    out=permuted[:, cols].rearrange("p (j m) -> p j m", j=PACK),
-                    in_=raw[:, cols].rearrange("p (m j) -> p j m", j=PACK),
-                )
+            nc.vector.tensor_copy(
+                out=permuted[:, cols].rearrange("p (j m) -> p j m", j=PACK),
+                in_=raw[:, cols].rearrange("p (m j) -> p j m", j=PACK),
+            )
 
         bias_cols = const.tile([P, OUT_TILES], BF16)
-        with nc.allow_non_contiguous_dma(reason="256 bias values, one per partition and tile"):
-            nc.sync.dma_start(out=bias_cols[:], in_=bias.rearrange("(t p) -> p t", p=P))
-
         x_rows = {}
 
-        def load_x(g):
-            for half in range(HALVES):
-                first = GROUP * g + HALF * half
-                rows = x_pool.tile([P, HALF // P, D], BF16, name="x_rows")
-                nc.sync.dma_start(
-                    out=rows[:], in_=xw[first : first + HALF, :].rearrange("(s p) d -> p s d", p=P)
-                )
-                x_rows[(g, half)] = rows
+        def x_pieces(g):
+            if g == 0:
+                return ((0, P), (P, P), (HALF, HALF))
+            return ((0, HALF), (HALF, HALF))
 
-        def load_stage1_weights(words, scales, first, count):
-            cols = slice(first, first + count)
+        def load_x(g, i):
+            first, count = x_pieces(g)[i]
+            start = GROUP * g + first
+            rows = x_pool.tile([P, HALF // P, D], BF16, name="x_rows")
             nc.sync.dma_start(
-                out=w1_words_raw[:, cols].rearrange("p (g n) -> p g n", g=TERMS),
-                in_=words.rearrange("g p n t -> p g (n t)").bitcast(I32),
+                out=rows[:, 0 : count // P, :],
+                in_=xw[start : start + count, :].rearrange("(s p) d -> p s d", p=P),
             )
+            x_rows[(g, i)] = rows
+
+        def load_stage1_words(words, terms, first):
+            count = (terms.stop - terms.start) * words.shape[2]
+            nc.sync.dma_start(
+                out=w1_words_raw[:, first : first + count].rearrange(
+                    "p (g n) -> p g n", n=words.shape[2]
+                ),
+                in_=words[terms].rearrange("g p n t -> p g (n t)").bitcast(I32),
+            )
+
+        def load_stage1_scales(scales, first, count):
+            cols = slice(first, first + count)
             for quadrant in range(QUADRANTS):
                 nc.sync.dma_start(
                     out=w1_scales_raw[32 * quadrant : 32 * quadrant + SCALE_ROWS, cols]
@@ -101,36 +109,47 @@ def tile_skconv2d_pa_t_e_kernel(
 
         w2_raw = const.tile([P, HIDDEN // P, OUT_CH], BF16)
 
-        load_x(0)
-        load_stage1_weights(S1s_words, S1s_scales, 0, H1)
-        load_x(1)
-        load_stage1_weights(U2s_words, U2s_scales, H1, HIDDEN - H1)
+        load_x(0, 0)
+        load_stage1_words(U2s_words, slice(0, TERMS // 2), 0)
+        load_stage1_scales(U2s_scales, 0, H2)
+        load_x(0, 1)
+        load_x(0, 2)
+        load_stage1_words(U2s_words, slice(TERMS // 2, TERMS), K_PASS)
+        load_stage1_words(S1s_words, slice(0, TERMS), H2)
+        load_stage1_scales(S1s_scales, H2, HIDDEN - H2)
+        load_x(1, 0)
+        load_x(1, 1)
         nc.sync.dma_start(
-            out=w2_raw[:, 0 : H1 // P, :],
-            in_=U1s.rearrange("t r o -> (t r) o").rearrange("(p j) o -> p j o", j=PACK),
-        )
-        nc.sync.dma_start(
-            out=w2_raw[:, H1 // P :, :].rearrange("p (c j) o -> p c j o", j=PACK),
+            out=w2_raw[:, 0 : H2 // P, :].rearrange("p (c j) o -> p c j o", j=PACK),
             in_=S2s.rearrange("t r o -> (t r) o").rearrange("(c p j) o -> p c j o", p=P, j=PACK),
         )
+        nc.sync.dma_start(
+            out=w2_raw[:, H2 // P :, :],
+            in_=U1s.rearrange("t r o -> (t r) o").rearrange("(p j) o -> p j o", j=PACK),
+        )
+        with nc.allow_non_contiguous_dma(reason="256 bias values, one per partition and tile"):
+            nc.sync.dma_start(out=bias_cols[:], in_=bias.rearrange("(t p) -> p t", p=P))
         for g in range(2, GROUPS):
-            load_x(g)
+            load_x(g, 0)
+            load_x(g, 1)
 
         bias2 = const.tile([P, OUT_TILES], F32)
-        nc.scalar.activation(out=bias2[:], in_=bias_cols[:], func=IDENTITY, scale=2.0)
 
         w2_grouped = const.tile([P, HIDDEN_PASSES, OUT_CH, PACK], BF16, align_bytes=64)
         w2_words = const.tile([P, HIDDEN_PASSES, OUT_CH], U32, align_bytes=64)
         w2_scales = const.tile([P, HIDDEN_PASSES, OUT_CH], U8, align_bytes=64)
 
-        def quantise_stage2_weights():
+        def prepare_stage2():
+            nc.scalar.activation(out=bias2[:], in_=bias_cols[:], func=IDENTITY, scale=2.0)
             for c in range(HIDDEN_PASSES):
-                copy = nc.scalar.copy if c < HIDDEN_PASSES - 1 else nc.vector.tensor_copy
-                copy(
+                nc.gpsimd.tensor_scalar(
                     out=w2_grouped[:, c],
-                    in_=w2_raw[:, PACK * c : PACK * (c + 1), :].rearrange("p j o -> p o j"),
+                    in0=w2_raw[:, PACK * c : PACK * (c + 1), :].rearrange("p j o -> p o j"),
+                    scalar1=1.0,
+                    scalar2=0.0,
+                    op0=MULT,
+                    op1=ADD,
                 )
-            for c in range(HIDDEN_PASSES):
                 nc.vector.quantize_mx(
                     out=w2_words[:, c, :].bitcast(FP8X4),
                     scales=w2_scales[:, c, :],
@@ -144,45 +163,51 @@ def tile_skconv2d_pa_t_e_kernel(
         h_words = {}
         h_scales = {}
 
-        def transpose_x(g):
-            grouped = pair.tile([P, GROUP * PACK], BF16, align_bytes=64, name="x_grouped")
-            grouped_words = grouped[:].bitcast(F32).rearrange("p (w u) -> p w u", u=2)
-            for half in range(HALVES):
-                xt = side_psum.tile([P, 2, HALF], F32, name="xt", tag="side")
-                for s in range(HALF // P):
-                    words = x_rows[(g, half)][:, s, :].bitcast(F32)
-                    for u in range(2):
-                        nc.tensor.transpose(
-                            xt[:, u, P * s : P * (s + 1)], words[:, u : D // 2 : 2], ident[:]
-                        )
-                nc.scalar.copy(
-                    out=grouped_words[:, HALF * half : HALF * (half + 1), :],
-                    in_=xt[:].rearrange("p u w -> p w u"),
-                )
-            x_grouped[g] = grouped
+        def transpose_x(g, i):
+            if i == 0:
+                x_grouped[g] = stage.tile([P, GROUP * PACK], BF16, align_bytes=64, name="x_grouped")
+            grouped_words = x_grouped[g][:].bitcast(F32).rearrange("p (w u) -> p w u", u=2)
+            first, count = x_pieces(g)[i]
+            xt = side_psum.tile([P, 2, count], F32, name="xt", tag="side")
+            for s in range(count // P):
+                words = x_rows[(g, i)][:, s, :].bitcast(F32)
+                for u in range(2):
+                    nc.tensor.transpose(
+                        xt[:, u, P * s : P * (s + 1)], words[:, u : D // 2 : 2], ident[:]
+                    )
+            copy = nc.vector.tensor_copy if (g, i) == (0, 2) else nc.scalar.copy
+            copy(
+                out=grouped_words[:, first : first + count, :],
+                in_=xt[:].rearrange("p u w -> p w u"),
+            )
 
-        def quantise_x(g):
-            words = pair.tile([P, GROUP], U32, align_bytes=64, name="x_words")
-            scales = pair.tile([P, GROUP], U8, align_bytes=64, name="x_scales")
-            for half in range(HALVES):
-                windows = slice(HALF * half, HALF * (half + 1))
-                nc.vector.quantize_mx(
-                    out=words[:, windows].bitcast(FP8X4),
-                    scales=scales[:, windows],
-                    in_=x_grouped[g][:, PACK * HALF * half : PACK * HALF * (half + 1)],
-                )
-            x_words[g] = words
-            x_scales[g] = scales
+        def quantise_x(g, i):
+            if i == 0:
+                x_words[g] = stage.tile([P, GROUP], U32, align_bytes=64, name="x_words")
+                x_scales[g] = stage.tile([P, GROUP], U8, align_bytes=64, name="x_scales")
+            first, count = x_pieces(g)[i]
+            windows = slice(first, first + count)
+            nc.vector.quantize_mx(
+                out=x_words[g][:, windows].bitcast(FP8X4),
+                scales=x_scales[g][:, windows],
+                in_=x_grouped[g][:, PACK * first : PACK * (first + count)],
+            )
 
-        def stage1(g, c):
-            grouped = hg_pool.tile([P, GROUP, PACK], BF16, align_bytes=64, name="h_grouped")
-            for q in range(PIECES):
-                windows = slice(PIECE * q, PIECE * (q + 1))
+        def stage1_pieces(g, c, pieces):
+            if pieces[0] == 0:
+                h_grouped[(g, c)] = hg_pool.tile(
+                    [P, GROUP, PACK], BF16, align_bytes=64, name="h_grouped"
+                )
+            h_banks = {}
+            for q in pieces:
                 h_bank = h_psum.tile([P, PACK, PIECE], F32, name="h_bank")
-                for j in range(PACK):
-                    rows = slice(K_PASS * c + P * j, K_PASS * c + P * (j + 1))
+                h_banks[q] = h_bank
+            for j in range(PACK):
+                rows = slice(K_PASS * c + P * j, K_PASS * c + P * (j + 1))
+                for q in pieces:
+                    windows = slice(PIECE * q, PIECE * (q + 1))
                     nc.tensor.matmul_mx(
-                        out=h_bank[:, j, :],
+                        out=h_banks[q][:, j, :],
                         lhsT=w1_words[:, rows].bitcast(FP8X4),
                         lhsT_scale=w1_scales[:, rows],
                         rhs=x_words[g][:, windows].bitcast(FP8X4),
@@ -190,23 +215,49 @@ def tile_skconv2d_pa_t_e_kernel(
                         start=True,
                         stop=True,
                     )
-                copy = nc.scalar.copy if q % 2 == 0 else nc.vector.tensor_copy
-                copy(out=grouped[:, windows, :], in_=h_bank[:].rearrange("p j w -> p w j"))
-            h_grouped[(g, c)] = grouped
+            for q in pieces:
+                on_vector = q % 2 == 1
+                if g == 0:
+                    on_vector = q == 1
+                elif g % 2 == 1 and (c, q) == (2, 3):
+                    on_vector = False
+                copy = nc.vector.tensor_copy if on_vector else nc.scalar.copy
+                windows = slice(PIECE * q, PIECE * (q + 1))
+                copy(
+                    out=h_grouped[(g, c)][:, windows, :],
+                    in_=h_banks[q][:].rearrange("p j w -> p w j"),
+                )
 
-        def quantise_h(g, c):
+        def stage1(g, c):
+            stage1_pieces(g, c, (0, 1))
+            stage1_pieces(g, c, (2, 3))
+
+        def quantise_h(g, c, half=None):
+            windows = slice(0, GROUP) if half is None else slice(HALF * half, HALF * (half + 1))
             if c == 0:
-                words = pair.tile([P, HIDDEN_PASSES, GROUP], U32, align_bytes=64, name="h_words")
-                scales = pair.tile([P, HIDDEN_PASSES, GROUP], U8, align_bytes=64, name="h_scales")
+                words = stage.tile([P, HIDDEN_PASSES, GROUP], U32, align_bytes=64, name="h_words")
+                scales = stage.tile([P, HIDDEN_PASSES, GROUP], U8, align_bytes=64, name="h_scales")
                 h_words[g] = words
                 h_scales[g] = scales
             nc.vector.quantize_mx(
-                out=h_words[g][:, c, :].bitcast(FP8X4),
-                scales=h_scales[g][:, c, :],
-                in_=h_grouped[(g, c)][:].rearrange("p w j -> p (w j)"),
+                out=h_words[g][:, c, windows].bitcast(FP8X4),
+                scales=h_scales[g][:, c, windows],
+                in_=h_grouped[(g, c)][:, windows, :].rearrange("p w j -> p (w j)"),
             )
 
         out_rows = out.rearrange("b o i j -> b o (i j)")
+
+        def stage2_pass(y_bank, g, t, c, windows):
+            channels = slice(P * t, P * (t + 1))
+            nc.tensor.matmul_mx(
+                out=y_bank[:],
+                lhsT=w2_words[:, c, channels].bitcast(FP8X4),
+                lhsT_scale=w2_scales[:, c, channels],
+                rhs=h_words[g][:, c, windows].bitcast(FP8X4),
+                rhs_scale=h_scales[g][:, c, windows],
+                start=(c == 0),
+                stop=(c == HIDDEN_PASSES - 1),
+            )
 
         def stage2(g, t):
             image = GROUP * g // IMAGE
@@ -214,46 +265,82 @@ def tile_skconv2d_pa_t_e_kernel(
             channels = slice(P * t, P * (t + 1))
             y_bank = side_psum.tile([P, GROUP], F32, name="y_bank", tag="side")
             for c in range(HIDDEN_PASSES):
-                nc.tensor.matmul_mx(
-                    out=y_bank[:],
-                    lhsT=w2_words[:, c, channels].bitcast(FP8X4),
-                    lhsT_scale=w2_scales[:, c, channels],
-                    rhs=h_words[g][:, c, :].bitcast(FP8X4),
-                    rhs_scale=h_scales[g][:, c, :],
-                    start=(c == 0),
-                    stop=(c == HIDDEN_PASSES - 1),
-                )
+                stage2_pass(y_bank, g, t, c, slice(0, GROUP))
             y_sb = y_pool.tile([P, GROUP], F32, name="y_sb")
             nc.scalar.activation(
                 out=y_sb[:], in_=y_bank[:], func=IDENTITY, bias=bias2[:, t : t + 1], scale=1.0 / TERMS
             )
             nc.sync.dma_start(out=out_rows[image, channels, first : first + GROUP], in_=y_sb[:])
 
-        transpose_x(0)
-        permute_stage1_weights(0)
-        quantise_x(0)
+        def finish_last_group(g):
+            image = GROUP * g // IMAGE
+            y_banks = {}
+            for half in range(2):
+                for t in range(OUT_TILES):
+                    pool, tag = ((h_psum, "h_bank"), (side_psum, "side"))[half]
+                    y_bank = pool.tile([P, HALF], F32, name="y_bank", tag=tag)
+                    for c in range(HIDDEN_PASSES - 1):
+                        stage2_pass(y_bank, g, t, c, slice(HALF * half, HALF * (half + 1)))
+                    y_banks[(half, t)] = y_bank
+            last = HIDDEN_PASSES - 1
+            for half in range(2):
+                quantise_h(g, last, half)
+                for t in range(OUT_TILES):
+                    stage2_pass(y_banks[(half, t)], g, t, last, slice(HALF * half, HALF * (half + 1)))
+            for half in range(2):
+                first = GROUP * g % IMAGE + HALF * half
+                for t in range(OUT_TILES):
+                    y_sb = y_pool.tile([P, GROUP], F32, name="y_sb")
+                    if t == 0:
+                        nc.scalar.activation(
+                            out=y_sb[:, 0:HALF], in_=y_banks[(half, t)][:], func=IDENTITY,
+                            bias=bias2[:, t : t + 1], scale=1.0 / TERMS,
+                        )
+                    else:
+                        nc.vector.tensor_scalar(
+                            out=y_sb[:, 0:HALF], in0=y_banks[(half, t)][:], scalar1=1.0 / TERMS,
+                            scalar2=bias2[:, t : t + 1], op0=MULT, op1=ADD,
+                        )
+                    nc.sync.dma_start(
+                        out=out_rows[image, P * t : P * (t + 1), first : first + HALF], in_=y_sb[:, 0:HALF]
+                    )
+
+        def permute_weights(c):
+            permute_columns(w1_words, w1_words_raw, c)
+            permute_columns(w1_scales, w1_scales_raw, c)
+
+        transpose_x(0, 0)
+        permute_weights(0)
+        quantise_x(0, 0)
+        transpose_x(0, 1)
+        quantise_x(0, 1)
+        transpose_x(0, 2)
+        quantise_x(0, 2)
+        stage1_pieces(0, 0, (0,))
+        stage1_pieces(0, 0, (1,))
+        permute_weights(1)
+        stage1_pieces(0, 0, (2,))
+        stage1_pieces(0, 0, (3,))
         for g in range(GROUPS):
-            stage1(g, 0)
-            if g == 0:
-                permute_stage1_weights(1)
             if g > 0:
+                stage1(g, 0)
                 quantise_h(g - 1, 2)
+                if g == 1:
+                    prepare_stage2()
+            else:
+                permute_weights(2)
             if g + 1 < GROUPS:
-                transpose_x(g + 1)
+                transpose_x(g + 1, 0)
+                transpose_x(g + 1, 1)
             stage1(g, 1)
-            if g == 0:
-                permute_stage1_weights(2)
             quantise_h(g, 0)
             if g + 1 < GROUPS:
-                quantise_x(g + 1)
+                quantise_x(g + 1, 0)
+                quantise_x(g + 1, 1)
             if g > 0:
                 stage2(g - 1, 0)
             stage1(g, 2)
             quantise_h(g, 1)
             if g > 0:
                 stage2(g - 1, 1)
-            else:
-                quantise_stage2_weights()
-        quantise_h(GROUPS - 1, 2)
-        stage2(GROUPS - 1, 0)
-        stage2(GROUPS - 1, 1)
+        finish_last_group(GROUPS - 1)

from contextlib import ExitStack

import concourse.mybir as mybir
from concourse.masks import make_identity

F32 = mybir.dt.float32
BF16 = mybir.dt.bfloat16
I32 = mybir.dt.int32
U32 = mybir.dt.uint32
U8 = mybir.dt.uint8
FP8X4 = mybir.dt.float8_e4m3fn_x4
IDENTITY = mybir.ActivationFunctionType.Identity
MULT = mybir.AluOpType.mult
ADD = mybir.AluOpType.add

P = 128
PACK = 4
K_PASS = P * PACK

WINDOWS = 4096
D = 512
TERMS = 8
H2 = 1024
HIDDEN = 1536
HIDDEN_PASSES = HIDDEN // K_PASS
OUT_CH = 256
OUT_TILES = OUT_CH // P
IMAGE = 1024

GROUP = 512
GROUPS = WINDOWS // GROUP
PIECE = 128
PIECES = GROUP // PIECE
HALF = GROUP // 2
SCALE_ROWS = 4
QUADRANTS = 4

FLOPS = 2 * WINDOWS * D * HIDDEN + 2 * WINDOWS * HIDDEN * OUT_CH


def tile_skconv2d_pa_t_e_kernel(
    tc, xw, S1s_words, S1s_scales, U1s, U2s_words, U2s_scales, S2s, bias, out
):
    nc = tc.nc
    with ExitStack() as ctx:
        const = ctx.enter_context(tc.tile_pool(name="const", bufs=1))
        x_pool = ctx.enter_context(tc.tile_pool(name="x_rows", bufs=2 * GROUPS + 1))
        stage = ctx.enter_context(tc.tile_pool(name="stage", bufs=4))
        hg_pool = ctx.enter_context(tc.tile_pool(name="h_grouped", bufs=9))
        y_pool = ctx.enter_context(tc.tile_pool(name="y", bufs=8))
        h_psum = ctx.enter_context(tc.psum_pool(name="h_psum", bufs=6))
        side_psum = ctx.enter_context(tc.psum_pool(name="side_psum", bufs=2))
        ctx.enter_context(tc.manual_schedule())

        ident = const.tile([P, P], F32)
        make_identity(nc, ident[:])

        w1_words_raw = const.tile([P, HIDDEN], I32, align_bytes=64)
        w1_scales_raw = const.tile([P, HIDDEN], U8, align_bytes=64)
        nc.vector.memset(w1_scales_raw[:].bitcast(I32), 0)
        w1_words = const.tile([P, HIDDEN], I32, align_bytes=64)
        w1_scales = const.tile([P, HIDDEN], U8, align_bytes=64)

        def permute_columns(permuted, raw, c):
            cols = slice(K_PASS * c, K_PASS * (c + 1))
            nc.vector.tensor_copy(
                out=permuted[:, cols].rearrange("p (j m) -> p j m", j=PACK),
                in_=raw[:, cols].rearrange("p (m j) -> p j m", j=PACK),
            )

        bias_cols = const.tile([P, OUT_TILES], BF16)
        x_rows = {}

        def x_pieces(g):
            if g == 0:
                return ((0, P), (P, P), (HALF, HALF))
            return ((0, HALF), (HALF, HALF))

        def load_x(g, i):
            first, count = x_pieces(g)[i]
            start = GROUP * g + first
            rows = x_pool.tile([P, HALF // P, D], BF16, name="x_rows")
            nc.sync.dma_start(
                out=rows[:, 0 : count // P, :],
                in_=xw[start : start + count, :].rearrange("(s p) d -> p s d", p=P),
            )
            x_rows[(g, i)] = rows

        def load_stage1_words(words, terms, first):
            count = (terms.stop - terms.start) * words.shape[2]
            nc.sync.dma_start(
                out=w1_words_raw[:, first : first + count].rearrange(
                    "p (g n) -> p g n", n=words.shape[2]
                ),
                in_=words[terms].rearrange("g p n t -> p g (n t)").bitcast(I32),
            )

        def load_stage1_scales(scales, first, count):
            cols = slice(first, first + count)
            for quadrant in range(QUADRANTS):
                nc.sync.dma_start(
                    out=w1_scales_raw[32 * quadrant : 32 * quadrant + SCALE_ROWS, cols]
                    .bitcast(I32)
                    .rearrange("r (g n) -> r g n", g=TERMS),
                    in_=scales[:, SCALE_ROWS * quadrant : SCALE_ROWS * (quadrant + 1), :]
                    .rearrange("g r n -> r g n")
                    .bitcast(I32),
                )

        w2_raw = const.tile([P, HIDDEN // P, OUT_CH], BF16)

        load_x(0, 0)
        load_stage1_words(U2s_words, slice(0, TERMS // 2), 0)
        load_stage1_scales(U2s_scales, 0, H2)
        load_x(0, 1)
        load_x(0, 2)
        load_stage1_words(U2s_words, slice(TERMS // 2, TERMS), K_PASS)
        load_stage1_words(S1s_words, slice(0, TERMS), H2)
        load_stage1_scales(S1s_scales, H2, HIDDEN - H2)
        load_x(1, 0)
        load_x(1, 1)
        nc.sync.dma_start(
            out=w2_raw[:, 0 : H2 // P, :].rearrange("p (c j) o -> p c j o", j=PACK),
            in_=S2s.rearrange("t r o -> (t r) o").rearrange("(c p j) o -> p c j o", p=P, j=PACK),
        )
        nc.sync.dma_start(
            out=w2_raw[:, H2 // P :, :],
            in_=U1s.rearrange("t r o -> (t r) o").rearrange("(p j) o -> p j o", j=PACK),
        )
        with nc.allow_non_contiguous_dma(reason="256 bias values, one per partition and tile"):
            nc.sync.dma_start(out=bias_cols[:], in_=bias.rearrange("(t p) -> p t", p=P))
        for g in range(2, GROUPS):
            load_x(g, 0)
            load_x(g, 1)

        bias2 = const.tile([P, OUT_TILES], F32)

        w2_grouped = const.tile([P, HIDDEN_PASSES, OUT_CH, PACK], BF16, align_bytes=64)
        w2_words = const.tile([P, HIDDEN_PASSES, OUT_CH], U32, align_bytes=64)
        w2_scales = const.tile([P, HIDDEN_PASSES, OUT_CH], U8, align_bytes=64)

        def prepare_stage2():
            nc.scalar.activation(out=bias2[:], in_=bias_cols[:], func=IDENTITY, scale=2.0)
            for c in range(HIDDEN_PASSES):
                nc.gpsimd.tensor_scalar(
                    out=w2_grouped[:, c],
                    in0=w2_raw[:, PACK * c : PACK * (c + 1), :].rearrange("p j o -> p o j"),
                    scalar1=1.0,
                    scalar2=0.0,
                    op0=MULT,
                    op1=ADD,
                )
                nc.vector.quantize_mx(
                    out=w2_words[:, c, :].bitcast(FP8X4),
                    scales=w2_scales[:, c, :],
                    in_=w2_grouped[:, c].rearrange("p o j -> p (o j)"),
                )

        x_grouped = {}
        x_words = {}
        x_scales = {}
        h_grouped = {}
        h_words = {}
        h_scales = {}

        def transpose_x(g, i):
            if i == 0:
                x_grouped[g] = stage.tile([P, GROUP * PACK], BF16, align_bytes=64, name="x_grouped")
            grouped_words = x_grouped[g][:].bitcast(F32).rearrange("p (w u) -> p w u", u=2)
            first, count = x_pieces(g)[i]
            xt = side_psum.tile([P, 2, count], F32, name="xt", tag="side")
            for s in range(count // P):
                words = x_rows[(g, i)][:, s, :].bitcast(F32)
                for u in range(2):
                    nc.tensor.transpose(
                        xt[:, u, P * s : P * (s + 1)], words[:, u : D // 2 : 2], ident[:]
                    )
            copy = nc.vector.tensor_copy if (g, i) == (0, 2) else nc.scalar.copy
            copy(
                out=grouped_words[:, first : first + count, :],
                in_=xt[:].rearrange("p u w -> p w u"),
            )

        def quantise_x(g, i):
            if i == 0:
                x_words[g] = stage.tile([P, GROUP], U32, align_bytes=64, name="x_words")
                x_scales[g] = stage.tile([P, GROUP], U8, align_bytes=64, name="x_scales")
            first, count = x_pieces(g)[i]
            windows = slice(first, first + count)
            nc.vector.quantize_mx(
                out=x_words[g][:, windows].bitcast(FP8X4),
                scales=x_scales[g][:, windows],
                in_=x_grouped[g][:, PACK * first : PACK * (first + count)],
            )

        def stage1_pieces(g, c, pieces):
            if pieces[0] == 0:
                h_grouped[(g, c)] = hg_pool.tile(
                    [P, GROUP, PACK], BF16, align_bytes=64, name="h_grouped"
                )
            h_banks = {}
            for q in pieces:
                h_bank = h_psum.tile([P, PACK, PIECE], F32, name="h_bank")
                h_banks[q] = h_bank
            for j in range(PACK):
                rows = slice(K_PASS * c + P * j, K_PASS * c + P * (j + 1))
                for q in pieces:
                    windows = slice(PIECE * q, PIECE * (q + 1))
                    nc.tensor.matmul_mx(
                        out=h_banks[q][:, j, :],
                        lhsT=w1_words[:, rows].bitcast(FP8X4),
                        lhsT_scale=w1_scales[:, rows],
                        rhs=x_words[g][:, windows].bitcast(FP8X4),
                        rhs_scale=x_scales[g][:, windows],
                        start=True,
                        stop=True,
                    )
            for q in pieces:
                on_vector = q % 2 == 1
                if g == 0:
                    on_vector = q == 1
                elif g % 2 == 1 and (c, q) == (2, 3):
                    on_vector = False
                copy = nc.vector.tensor_copy if on_vector else nc.scalar.copy
                windows = slice(PIECE * q, PIECE * (q + 1))
                copy(
                    out=h_grouped[(g, c)][:, windows, :],
                    in_=h_banks[q][:].rearrange("p j w -> p w j"),
                )

        def stage1(g, c):
            stage1_pieces(g, c, (0, 1))
            stage1_pieces(g, c, (2, 3))

        def quantise_h(g, c, half=None):
            windows = slice(0, GROUP) if half is None else slice(HALF * half, HALF * (half + 1))
            if c == 0:
                words = stage.tile([P, HIDDEN_PASSES, GROUP], U32, align_bytes=64, name="h_words")
                scales = stage.tile([P, HIDDEN_PASSES, GROUP], U8, align_bytes=64, name="h_scales")
                h_words[g] = words
                h_scales[g] = scales
            nc.vector.quantize_mx(
                out=h_words[g][:, c, windows].bitcast(FP8X4),
                scales=h_scales[g][:, c, windows],
                in_=h_grouped[(g, c)][:, windows, :].rearrange("p w j -> p (w j)"),
            )

        out_rows = out.rearrange("b o i j -> b o (i j)")

        def stage2_pass(y_bank, g, t, c, windows):
            channels = slice(P * t, P * (t + 1))
            nc.tensor.matmul_mx(
                out=y_bank[:],
                lhsT=w2_words[:, c, channels].bitcast(FP8X4),
                lhsT_scale=w2_scales[:, c, channels],
                rhs=h_words[g][:, c, windows].bitcast(FP8X4),
                rhs_scale=h_scales[g][:, c, windows],
                start=(c == 0),
                stop=(c == HIDDEN_PASSES - 1),
            )

        def stage2(g, t):
            image = GROUP * g // IMAGE
            first = GROUP * g % IMAGE
            channels = slice(P * t, P * (t + 1))
            y_bank = side_psum.tile([P, GROUP], F32, name="y_bank", tag="side")
            for c in range(HIDDEN_PASSES):
                stage2_pass(y_bank, g, t, c, slice(0, GROUP))
            y_sb = y_pool.tile([P, GROUP], F32, name="y_sb")
            nc.scalar.activation(
                out=y_sb[:], in_=y_bank[:], func=IDENTITY, bias=bias2[:, t : t + 1], scale=1.0 / TERMS
            )
            nc.sync.dma_start(out=out_rows[image, channels, first : first + GROUP], in_=y_sb[:])

        def finish_last_group(g):
            image = GROUP * g // IMAGE
            y_banks = {}
            for half in range(2):
                for t in range(OUT_TILES):
                    pool, tag = ((h_psum, "h_bank"), (side_psum, "side"))[half]
                    y_bank = pool.tile([P, HALF], F32, name="y_bank", tag=tag)
                    for c in range(HIDDEN_PASSES - 1):
                        stage2_pass(y_bank, g, t, c, slice(HALF * half, HALF * (half + 1)))
                    y_banks[(half, t)] = y_bank
            last = HIDDEN_PASSES - 1
            for half in range(2):
                quantise_h(g, last, half)
                for t in range(OUT_TILES):
                    stage2_pass(y_banks[(half, t)], g, t, last, slice(HALF * half, HALF * (half + 1)))
            for half in range(2):
                first = GROUP * g % IMAGE + HALF * half
                for t in range(OUT_TILES):
                    y_sb = y_pool.tile([P, GROUP], F32, name="y_sb")
                    if t == 0:
                        nc.scalar.activation(
                            out=y_sb[:, 0:HALF], in_=y_banks[(half, t)][:], func=IDENTITY,
                            bias=bias2[:, t : t + 1], scale=1.0 / TERMS,
                        )
                    else:
                        nc.vector.tensor_scalar(
                            out=y_sb[:, 0:HALF], in0=y_banks[(half, t)][:], scalar1=1.0 / TERMS,
                            scalar2=bias2[:, t : t + 1], op0=MULT, op1=ADD,
                        )
                    nc.sync.dma_start(
                        out=out_rows[image, P * t : P * (t + 1), first : first + HALF], in_=y_sb[:, 0:HALF]
                    )

        def permute_weights(c):
            permute_columns(w1_words, w1_words_raw, c)
            permute_columns(w1_scales, w1_scales_raw, c)

        transpose_x(0, 0)
        permute_weights(0)
        quantise_x(0, 0)
        transpose_x(0, 1)
        quantise_x(0, 1)
        transpose_x(0, 2)
        quantise_x(0, 2)
        stage1_pieces(0, 0, (0,))
        stage1_pieces(0, 0, (1,))
        permute_weights(1)
        stage1_pieces(0, 0, (2,))
        stage1_pieces(0, 0, (3,))
        for g in range(GROUPS):
            if g > 0:
                stage1(g, 0)
                quantise_h(g - 1, 2)
                if g == 1:
                    prepare_stage2()
            else:
                permute_weights(2)
            if g + 1 < GROUPS:
                transpose_x(g + 1, 0)
                transpose_x(g + 1, 1)
            stage1(g, 1)
            quantise_h(g, 0)
            if g + 1 < GROUPS:
                quantise_x(g + 1, 0)
                quantise_x(g + 1, 1)
            if g > 0:
                stage2(g - 1, 0)
            stage1(g, 2)
            quantise_h(g, 1)
            if g > 0:
                stage2(g - 1, 1)
        finish_last_group(GROUPS - 1)
